import numpy as np
import ml_dtypes


def mxq(x, axis, fmt="e4m3"):
    dtype, down = {"e4m3": (ml_dtypes.float8_e4m3fn, 7), "e5m2": (ml_dtypes.float8_e5m2, 14)}[fmt]
    v = np.moveaxis(np.asarray(x, np.float32).astype(ml_dtypes.bfloat16).astype(np.float64), axis, -1)
    blocks = v.reshape(v.shape[:-1] + (-1, 32))
    amax = np.abs(blocks).max(-1, keepdims=True)
    byte = np.maximum(np.where(amax > 0, np.frexp(amax)[1] - 1 + 127, 0) - down, 1)
    scale = np.exp2(byte - 127.0)
    codes = (blocks / scale).astype(np.float32).astype(dtype).astype(np.float64)
    return np.moveaxis((codes * scale).reshape(v.shape), -1, axis)


WIDE = False


def mx_kscale(k):
    if not WIDE:
        return np.ones(k)
    levels = np.array([10, -10, 5, -5, 0])
    if k % 512:
        return np.exp2(np.random.permutation(np.resize(levels, k // 32))).repeat(32)
    a = np.empty((k // 512, 16))
    for p in range(k // 512):
        a[p, :8] = np.random.permutation(np.resize(levels, 8))
        for g in range(8):
            far = levels[np.abs(levels - a[p, g]) >= 10]
            a[p, g + 8] = far[np.random.randint(len(far))]
    return np.exp2(a.ravel()).repeat(32)


BF16 = ml_dtypes.bfloat16


def bf(x):
    return np.asarray(x, np.float32).astype(BF16)


def f64(x):
    return np.asarray(x).astype(np.float64)


B, T, DIM, DQ, H = 1, 512, 2048, 2048, 16
HD = DQ // H
HP = HD // 2
EPS = 1e-6


def rmsnorm(t, g):
    return g * (t * (1.0 / np.sqrt(np.mean(t * t, axis=-1, keepdims=True) + EPS)))


def rope(t, ang):
    b, n, h, d = t.shape
    tp = t.reshape(b, n, h, d // 2, 2)
    cos = np.cos(ang)[None, :, None, :]
    sin = np.sin(ang)[None, :, None, :]
    x0, x1 = tp[..., 0], tp[..., 1]
    return np.stack([x0 * cos - x1 * sin, x0 * sin + x1 * cos], axis=-1).reshape(b, n, h, d)


def draw0():
    s = mx_kscale(DIM)
    w = 1.0 / np.sqrt(DIM)
    return {"x": bf(np.random.standard_normal((B, T, DIM)) * s),
            "freqs": bf(np.random.uniform(-np.pi, np.pi, (T, HP))),
            "Wq": bf(np.random.standard_normal((DIM, DQ)) * w / s[:, None]),
            "bq": bf(np.random.standard_normal(DQ) * 0.3),
            "Wk": bf(np.random.standard_normal((DIM, DQ)) * w / s[:, None]),
            "bk": bf(np.random.standard_normal(DQ) * 0.3),
            "gq": bf(1.0 + 0.1 * np.random.standard_normal(DQ)),
            "gk": bf(1.0 + 0.1 * np.random.standard_normal(DQ))}


def core(x, freqs, Wq, bq, Wk, bk, gq, gk):
    xq = mxq(f64(x), 2, "e4m3")
    q = rmsnorm((xq @ mxq(f64(Wq), 0, "e4m3")) + f64(bq), f64(gq))
    k = rmsnorm((xq @ mxq(f64(Wk), 0, "e4m3")) + f64(bk), f64(gk))
    ang = f64(freqs)
    return rope(q.reshape(B, T, H, HD), ang), rope(k.reshape(B, T, H, HD), ang)


def e4m3fn_bytes(y):
    return np.clip(np.asarray(y, np.float64), -448.0, 448.0).astype(np.float32).astype(ml_dtypes.float8_e4m3fn).view(np.uint8)


def e4m3fn_values(b):
    return np.asarray(b, np.uint8).view(ml_dtypes.float8_e4m3fn).astype(np.float64)


def setup_inputs():
    d = draw0()
    x0 = np.asarray(d['Wq']).astype(np.float64)
    s = (np.max(np.abs(x0), axis=(1,), keepdims=True) / 448.0).astype(np.float32)
    out = {}
    for k, v in d.items():
        if k == 'Wq':
            out['Wq_bytes'] = e4m3fn_bytes(x0 / s.astype(np.float64))
            out['Wq_scale'] = s
        else:
            out[k] = v
    return out


def reference(x, freqs, Wq_bytes, Wq_scale, bq, Wk, bk, gq, gk):
    return core(x, freqs, e4m3fn_values(Wq_bytes) * Wq_scale.astype(np.float64), bq, Wk, bk, gq, gk)

@@ -1,0 +1,394 @@
+from contextlib import ExitStack
+
+import concourse.mybir as mybir
+from concourse.masks import make_identity
+
+F32 = mybir.dt.float32
+BF16 = mybir.dt.bfloat16
+U32 = mybir.dt.uint32
+U8 = mybir.dt.uint8
+FP8 = mybir.dt.float8_e4m3fn
+FP8X4 = mybir.dt.float8_e4m3fn_x4
+ACT = mybir.ActivationFunctionType
+ALU = mybir.AluOpType
+AX = mybir.AxisListType
+
+T = 512
+DIM = 2048
+DQ = 2048
+H = 16
+EPS = 1e-6
+HALF_PI = 1.5707963267948966
+P = 128
+PACK = 4
+G = DIM // (P * PACK)
+TB = T // P
+CW = 512
+HC = CW // P
+NCH = DQ // CW
+UNITS = 2 * NCH * G
+HEADS = 2 * H
+
+FLOPS = 2 * T * DIM * 2 * DQ
+
+LAG_PROJECT = 4
+LAG_READ = 5
+LAG_SQUARES = 8
+FIRST_ROTATE = 20
+OB_BANKS = 3
+K_ON_SCALAR = 5
+X_ON_SCALAR = 2
+WV_EARLY = 3
+WV_LATE = 2
+ROTS = 8
+SLABS = 6
+
+
+def tile_causalselfattention_pa_kernel(
+    tc, x, freqs, Wq_bytes, Wq_scale, bq, Wk, bk, gq, gk, out_0, out_1
+):
+    nc = tc.nc
+    with ExitStack() as ctx:
+        const = ctx.enter_context(tc.tile_pool(name="const", bufs=1))
+        slab = ctx.enter_context(tc.tile_pool(name="slab", bufs=SLABS))
+        rpool = ctx.enter_context(tc.tile_pool(name="rpool", bufs=ROTS))
+        qpool = ctx.enter_context(tc.tile_pool(name="qpool", bufs=8))
+        kpool = ctx.enter_context(tc.tile_pool(name="kpool", bufs=8))
+        stage = ctx.enter_context(tc.tile_pool(name="stage", bufs=3))
+        cpool = ctx.enter_context(tc.tile_pool(name="cpool", bufs=3))
+        spool = ctx.enter_context(tc.tile_pool(name="spool", bufs=5))
+        opool = ctx.enter_context(tc.tile_pool(name="opool", bufs=8))
+        ps_acc = ctx.enter_context(tc.psum_pool(name="ps_acc", bufs=4))
+        ps_ob = ctx.enter_context(tc.psum_pool(name="ps_ob", bufs=OB_BANKS))
+        ps_ss = ctx.enter_context(tc.psum_pool(name="ps_ss", bufs=1))
+
+        q_view = Wq_bytes.rearrange("(g p j) n -> g p j n", p=P, j=PACK)
+        k_view = Wk.rearrange("(g p j) n -> g p j n", p=P, j=PACK)
+        x_view = x.rearrange("o (b t) k -> t (o b) k", t=P)
+        out_views = (
+            out_0.rearrange("o t h d -> (o t) (h d)"),
+            out_1.rearrange("o t h d -> (o t) (h d)"),
+        )
+
+        raw = {}
+        wide = {}
+        grouped = {}
+        codes = {}
+        ys = {}
+        sqs = {}
+        rots = {}
+        sums = {}
+        obs = {}
+        accs = {}
+
+        def unit_place(u):
+            return u // (NCH * G), (u // G) % NCH, u % G
+
+        def load(u):
+            w, c, g = unit_place(u)
+            ns = slice(c * CW, (c + 1) * CW)
+            if w == 0:
+                t = qpool.tile([P, PACK, CW], U8, name="wq_bytes_sb", tag="wq_bytes_sb")
+                nc.sync.dma_start(out=t[:], in_=q_view[g][:, :, ns])
+            else:
+                t = kpool.tile([P, PACK, CW], BF16, name="wk_sb", tag="wk_sb")
+                nc.sync.dma_start(out=t[:], in_=k_view[g][:, :, ns])
+            raw[u] = t
+
+        def widen_on_vector(u, j):
+            if u == 0:
+                return True
+            share = WV_EARLY if u < FIRST_ROTATE else WV_LATE
+            return j >= PACK - (share + u % 2) // 2
+
+        def widen(u):
+            w, c, g = unit_place(u)
+            t = stage.tile([P, PACK, CW], BF16, name="wide", tag="wide")
+            for j in range(PACK):
+                src = raw[u][:, j, :].bitcast(FP8)
+                sc = wsc[g][:, j : j + 1]
+                if widen_on_vector(u, j):
+                    nc.vector.tensor_scalar(
+                        out=t[:, j, :], in0=src, scalar1=sc, scalar2=None, op0=ALU.mult
+                    )
+                else:
+                    nc.scalar.activation(out=t[:, j, :], in_=src, func=ACT.Copy, scale=sc)
+            wide[u] = t
+
+        def interleave(u):
+            w, c, g = unit_place(u)
+            src = wide[u] if w == 0 else raw[u]
+            t = stage.tile([P, CW, PACK], BF16, name="grouped", tag="grouped", align_bytes=64)
+            dst_v = t[:].rearrange("p (c i) j -> p c j i", i=4)
+            src_v = src[:].rearrange("p j (c i) -> p c j i", i=4)
+            if w == 1 and ((u % 16 + 1) * K_ON_SCALAR) % 16 < K_ON_SCALAR:
+                nc.scalar.copy(out=dst_v, in_=src_v)
+            else:
+                nc.vector.tensor_copy(out=dst_v, in_=src_v)
+            grouped[u] = t
+
+        def quantize(u):
+            w, c, g = unit_place(u)
+            if g == 0:
+                wc = cpool.tile([P, G, CW], U32, name="w_codes", tag="w_codes", align_bytes=64)
+                ws = cpool.tile([P, G, CW], U8, name="w_scales", tag="w_scales", align_bytes=64)
+                codes[(w, c)] = (wc, ws)
+            wc, ws = codes[(w, c)]
+            nc.vector.quantize_mx(
+                out=wc[:, g, :].bitcast(FP8X4),
+                scales=ws[:, g, :],
+                in_=grouped[u][:].rearrange("p n j -> p (n j)"),
+            )
+
+        def project(hh):
+            w, h = hh // H, hh % H
+            c, hl = h // HC, h % HC
+            wc, ws = codes[(w, c)]
+            cs = slice(hl * P, (hl + 1) * P)
+            acc = ps_acc.tile([P, T], F32, name="acc", tag="acc")
+            for g in range(G):
+                nc.tensor.matmul_mx(
+                    out=acc[:],
+                    lhsT=wc[:, g, cs].bitcast(FP8X4),
+                    lhsT_scale=ws[:, g, cs],
+                    rhs=xc[:, g, :].bitcast(FP8X4),
+                    rhs_scale=xs[:, g, :],
+                    start=(g == 0),
+                    stop=(g == G - 1),
+                )
+            accs[hh] = acc
+
+        def read_bank(hh):
+            w, h = hh // H, hh % H
+            c, hl = h // HC, h % HC
+            acc = accs[hh]
+            sq = spool.tile([P, T], F32, name="sq", tag="sq")
+            nc.scalar.activation(
+                out=sq[:], in_=acc[:], func=ACT.Square, scale=1.0, bias=cols[:, hh : hh + 1]
+            )
+            if hl == 0:
+                ys[(w, c)] = slab.tile([P, HC, T], F32, name="y", tag="slab", align_bytes=64)
+            nc.scalar.activation(
+                out=ys[(w, c)][:, hl, :], in_=acc[:], func=ACT.Identity,
+                scale=cols[:, 2 * H + hh : 2 * H + hh + 1], bias=gb[:, hh : hh + 1],
+            )
+            sqs[hh] = sq
+
+        def rotate(r):
+            w, c, tb = r // (NCH * TB), (r // TB) % NCH, r % TB
+            ts = slice(tb * P, (tb + 1) * P)
+            rot = rpool.tile([P, HC, 2, P], F32, name="rot", tag="rot")
+            nc.vector.tensor_tensor(
+                out=rot[:],
+                in0=ys[(w, c)][:, :, ts].unsqueeze(2).to_broadcast([P, HC, 2, P]),
+                in1=tab[:, :, ts].unsqueeze(1).to_broadcast([P, HC, 2, P]),
+                op=ALU.mult,
+            )
+            rots[r] = rot
+
+        def add_squares(hh):
+            w, h = hh // H, hh % H
+            if h == 0:
+                sums[w] = ps_ss.tile([P, TB, P], F32, name="ss", tag="ss")
+            for tb in range(TB):
+                nc.tensor.matmul(
+                    out=sums[w][:, tb, :],
+                    lhsT=sqs[hh][:, tb * P : (tb + 1) * P],
+                    rhs=ident[:],
+                    is_transpose=True,
+                    start=(h == 0 and tb == 0),
+                    stop=(h == H - 1 and tb == TB - 1),
+                )
+
+        def norm(w):
+            for tb in range(TB):
+                nc.scalar.activation(
+                    out=junk[:], in_=sums[w][:, tb, :], func=ACT.Copy,
+                    accum_out=ssr[:, w * TB + tb : w * TB + tb + 1],
+                )
+            span = slice(w * TB, (w + 1) * TB)
+            nc.scalar.activation(
+                out=rstd[:, span], in_=ssr[:, span], func=ACT.Abs_reciprocal_sqrt,
+                scale=1.0 / DQ, bias=EPS,
+            )
+
+        def turn(r):
+            w, c, tb = r // (NCH * TB), (r // TB) % NCH, r % TB
+            rot = rots[r]
+            ob = ps_ob.tile([P, CW], F32, name="ob", tag="ob")
+            for hl in range(HC):
+                dst = ob[:, hl * P : (hl + 1) * P]
+                nc.tensor.matmul(
+                    out=dst, lhsT=rot[:, hl, 0, :], rhs=ident[:],
+                    is_transpose=True, start=True, stop=False,
+                )
+                nc.tensor.matmul(
+                    out=dst, lhsT=rot[:, hl, 1, :], rhs=swap[:],
+                    is_transpose=True, start=False, stop=True,
+                )
+            obs[r] = ob
+
+        def finish(r):
+            w, c, tb = r // (NCH * TB), (r // TB) % NCH, r % TB
+            o = opool.tile([P, CW], F32, name="osb", tag="osb")
+            rs = rstd[:, w * TB + tb : w * TB + tb + 1]
+            if r >= 28 and r % 2 == 1:
+                nc.vector.tensor_scalar(
+                    out=o[:], in0=obs[r][:], scalar1=rs, scalar2=None, op0=ALU.mult
+                )
+            else:
+                nc.scalar.activation(out=o[:], in_=obs[r][:], func=ACT.Copy, scale=rs)
+            nc.sync.dma_start(
+                out=out_views[w][tb * P : (tb + 1) * P, c * CW : (c + 1) * CW], in_=o[:]
+            )
+
+        warm = const.tile([P, 1], F32, name="warm", tag="warm")
+        nc.vector.memset(warm[:], 0.0)
+        nc.scalar.activation(out=warm[:], in_=warm[:], func=ACT.Sin)
+        wsc = []
+        s_view = Wq_scale.rearrange("(g p j) o -> g p (j o)", p=P, j=PACK)
+        for u in range(4):
+            wsc_g = const.tile([P, 2 * PACK], F32, name="wsc", tag="wsc%d" % u)
+            nc.sync.dma_start(out=wsc_g[:, 0:PACK], in_=s_view[u])
+            wsc.append(wsc_g)
+            load(u)
+        xr = []
+        for half in range(2):
+            xr_t = slab.tile([P, 2, DIM], BF16, name="x_raw", tag="slab", align_bytes=64)
+            xr.append(xr_t)
+            for b in range(2):
+                nc.sync.dma_start(out=xr_t[:, b, :], in_=x_view[:, 2 * half + b, :])
+        fr = const.tile([P, TB, 64], BF16, name="fr", tag="fr")
+        nc.sync.dma_start(out=fr[:], in_=freqs.rearrange("(b t) j -> t b j", t=P))
+        vb = const.tile([P, P], BF16, name="vb", tag="vb")
+        nc.vector.memset(vb[:], 0.0)
+        for v, vec in enumerate((bq, bk, gq, gk)):
+            nc.sync.dma_start(
+                out=vb[H * v : H * (v + 1), :], in_=vec.rearrange("(h c) -> h c", c=P)
+            )
+        for u in range(4, 8):
+            load(u)
+
+        ident = const.tile([P, P], F32, name="ident", tag="ident")
+        make_identity(nc, ident[:])
+        swap = const.tile([P, P], F32, name="swap", tag="swap")
+        iv = ident[:].rearrange("p (j e) -> p j e", e=2)
+        sv = swap[:].rearrange("p (j e) -> p j e", e=2)
+        nc.vector.tensor_copy(out=sv[:, :, 0], in_=iv[:, :, 1])
+        nc.vector.tensor_copy(out=sv[:, :, 1], in_=iv[:, :, 0])
+
+        af = const.tile([P, TB, 64], F32, name="af", tag="af")
+        ca = const.tile([P, TB, 64, 2], F32, name="ca", tag="ca")
+        sa = const.tile([P, TB, 64, 2], F32, name="sa", tag="sa")
+        nc.scalar.activation(out=af[:], in_=fr[:], func=ACT.Abs)
+        for e in range(2):
+            nc.scalar.activation(
+                out=ca[:, :, :, e], in_=af[:], func=ACT.Sin, scale=-1.0, bias=HALF_PI
+            )
+            nc.scalar.activation(
+                out=sa[:, :, :, e], in_=fr[:], func=ACT.Sin, scale=(1.0 if e == 0 else -1.0)
+            )
+
+        xc = const.tile([P, G, T], U32, name="x_codes", tag="x_codes", align_bytes=64)
+        xs = const.tile([P, G, T], U8, name="x_scales", tag="x_scales", align_bytes=64)
+        for g in range(G):
+            if g % 2 == 0:
+                xg = slab.tile([P, 2, PACK * T], BF16, name="x_grouped", tag="slab", align_bytes=64)
+            for pair in range(2):
+                xt = ps_ob.tile([P, 2, 2, P], F32, name="xt", tag="ob")
+                for b in range(2):
+                    words = xr[pair][:, b, :].bitcast(F32)
+                    for uu in range(2):
+                        nc.tensor.transpose(
+                            xt[:, b, uu, :], words[:, 256 * g + uu : 256 * (g + 1) : 2], ident[:]
+                        )
+                dst = xg[:, g % 2, :].bitcast(F32).rearrange("p (b t u) -> p b t u", b=TB, u=2)
+                dst = dst[:, 2 * pair : 2 * pair + 2, :, :]
+                src = xt[:].rearrange("p b u t -> p b t u")
+                if pair >= X_ON_SCALAR:
+                    nc.vector.tensor_copy(out=dst, in_=src)
+                else:
+                    nc.scalar.copy(out=dst, in_=src)
+            nc.vector.quantize_mx(
+                out=xc[:, g, :].bitcast(FP8X4), scales=xs[:, g, :], in_=xg[:, g % 2, :]
+            )
+
+        vf = const.tile([P, P], F32, name="vf", tag="vf")
+        nc.vector.tensor_copy(out=vf[:], in_=vb[:])
+        vp = ps_ob.tile([P, CW], F32, name="vp", tag="ob")
+        nc.tensor.transpose(vp[:, 0:P], vf[:], ident[:])
+        cols = const.tile([P, 4 * H], F32, name="cols", tag="cols")
+        nc.vector.tensor_copy(out=cols[:], in_=vp[:, 0 : 4 * H])
+        gb = const.tile([P, 2 * H], F32, name="gb", tag="gb")
+        nc.vector.tensor_tensor(
+            out=gb[:], in0=cols[:, 2 * H : 4 * H], in1=cols[:, 0 : 2 * H], op=ALU.mult
+        )
+
+        tab = const.tile([P, 2, T], F32, name="tab", tag="tab")
+        for s, src_t in enumerate((ca, sa)):
+            tp = ps_ob.tile([P, T], F32, name="tp", tag="ob")
+            for tb in range(TB):
+                nc.tensor.transpose(
+                    tp[:, tb * P : (tb + 1) * P],
+                    src_t[:, tb, :, :].rearrange("p j e -> p (j e)"),
+                    ident[:],
+                )
+            nc.scalar.copy(out=tab[:, s, :], in_=tp[:])
+
+        rstd = const.tile([P, 2 * TB], F32, name="rstd", tag="rstd")
+        ssr = const.tile([P, 2 * TB], F32, name="ssr", tag="ssr")
+        junk = const.tile([P, P], F32, name="junk", tag="junk")
+
+        n_norm = (H - 2 + LAG_SQUARES + 1, HEADS - 2 + LAG_SQUARES + 1)
+        n_units_out = NCH * TB
+        rotate_at = {}
+        turn_at = {}
+        finish_at = {}
+        last = 0
+        for r0 in range(0, 2 * n_units_out, 2):
+            w = r0 // n_units_out
+            for r in (r0, r0 + 1):
+                n_r = max(FIRST_ROTATE + r, (r // TB) * HC + HC + LAG_READ)
+                rotate_at.setdefault(n_r, []).append(r)
+            n_t = max(n_r + 1, n_norm[w] - OB_BANKS + (r0 + 1) % n_units_out)
+            n_t += n_t % 2
+            turn_at.setdefault(n_t, []).extend((r0, r0 + 1))
+            for r in (r0, r0 + 1):
+                n_f = max(n_t + 1 + r - r0, n_norm[w])
+                finish_at.setdefault(n_f, []).append(r)
+                last = max(last, n_f)
+        pinned = {mybir.EngineType.PE, mybir.EngineType.DVE, mybir.EngineType.Activation}
+        with tc.manual_schedule(engines=pinned):
+            widen(0)
+            widen(1)
+            interleave(0)
+            for n in range(last + 1):
+                if n + 8 < 16:
+                    load(n + 8)
+                if n < 8:
+                    load(16 + n)
+                if 16 <= n < 24:
+                    load(n + 8)
+                if n + 2 < 16:
+                    widen(n + 2)
+                if n + 1 < UNITS:
+                    interleave(n + 1)
+                for w in range(2):
+                    if n == n_norm[w]:
+                        norm(w)
+                for r in finish_at.get(n, []):
+                    finish(r)
+                for r in turn_at.get(n, []):
+                    turn(r)
+                if n % 2 == 0 and 0 <= n - LAG_SQUARES < HEADS:
+                    add_squares(n - LAG_SQUARES)
+                    add_squares(n - LAG_SQUARES + 1)
+                if n % 2 == 0 and 0 <= n - LAG_PROJECT < HEADS:
+                    project(n - LAG_PROJECT)
+                    project(n - LAG_PROJECT + 1)
+                if 0 <= n - LAG_READ < HEADS:
+                    read_bank(n - LAG_READ)
+                for r in rotate_at.get(n, []):
+                    rotate(r)
+                if n < UNITS:
+                    quantize(n)

@@ -34,13 +34,14 @@ FLOPS = 2 * T * DIM * 2 * DQ
 LAG_PROJECT = 4
 LAG_READ = 5
 LAG_SQUARES = 8
-FIRST_ROTATE = 20
+FIRST_ROTATE = 21
 OB_BANKS = 3
-K_ON_SCALAR = 5
+K_ON_SCALAR = 4
 X_ON_SCALAR = 2
 WV_EARLY = 3
 WV_LATE = 2
 ROTS = 8
+SINES_AT = 18
 SLABS = 6
 
 
@@ -277,18 +278,6 @@ def tile_causalselfattention_pa_kernel(
         nc.vector.tensor_copy(out=sv[:, :, 0], in_=iv[:, :, 1])
         nc.vector.tensor_copy(out=sv[:, :, 1], in_=iv[:, :, 0])
 
-        af = const.tile([P, TB, 64], F32, name="af", tag="af")
-        ca = const.tile([P, TB, 64, 2], F32, name="ca", tag="ca")
-        sa = const.tile([P, TB, 64, 2], F32, name="sa", tag="sa")
-        nc.scalar.activation(out=af[:], in_=fr[:], func=ACT.Abs)
-        for e in range(2):
-            nc.scalar.activation(
-                out=ca[:, :, :, e], in_=af[:], func=ACT.Sin, scale=-1.0, bias=HALF_PI
-            )
-            nc.scalar.activation(
-                out=sa[:, :, :, e], in_=fr[:], func=ACT.Sin, scale=(1.0 if e == 0 else -1.0)
-            )
-
         xc = const.tile([P, G, T], U32, name="x_codes", tag="x_codes", align_bytes=64)
         xs = const.tile([P, G, T], U8, name="x_scales", tag="x_scales", align_bytes=64)
         for g in range(G):
@@ -324,16 +313,31 @@ def tile_causalselfattention_pa_kernel(
             out=gb[:], in0=cols[:, 2 * H : 4 * H], in1=cols[:, 0 : 2 * H], op=ALU.mult
         )
 
+        af = const.tile([P, TB, 64], F32, name="af", tag="af")
+        ca = const.tile([P, TB, 64, 2], F32, name="ca", tag="ca")
+        sa = const.tile([P, TB, 64, 2], F32, name="sa", tag="sa")
         tab = const.tile([P, 2, T], F32, name="tab", tag="tab")
-        for s, src_t in enumerate((ca, sa)):
-            tp = ps_ob.tile([P, T], F32, name="tp", tag="ob")
-            for tb in range(TB):
-                nc.tensor.transpose(
-                    tp[:, tb * P : (tb + 1) * P],
-                    src_t[:, tb, :, :].rearrange("p j e -> p (j e)"),
-                    ident[:],
+
+        def sines():
+            nc.scalar.activation(out=af[:], in_=fr[:], func=ACT.Abs)
+            for e in range(2):
+                nc.scalar.activation(
+                    out=ca[:, :, :, e], in_=af[:], func=ACT.Sin, scale=-1.0, bias=HALF_PI
                 )
-            nc.scalar.copy(out=tab[:, s, :], in_=tp[:])
+                nc.scalar.activation(
+                    out=sa[:, :, :, e], in_=fr[:], func=ACT.Sin, scale=(1.0 if e == 0 else -1.0)
+                )
+
+        def tables():
+            for s, src_t in enumerate((ca, sa)):
+                tp = ps_ob.tile([P, T], F32, name="tp", tag="ob")
+                for tb in range(TB):
+                    nc.tensor.transpose(
+                        tp[:, tb * P : (tb + 1) * P],
+                        src_t[:, tb, :, :].rearrange("p j e -> p (j e)"),
+                        ident[:],
+                    )
+                nc.scalar.copy(out=tab[:, s, :], in_=tp[:])
 
         rstd = const.tile([P, 2 * TB], F32, name="rstd", tag="rstd")
         ssr = const.tile([P, 2 * TB], F32, name="ssr", tag="ssr")
@@ -369,6 +373,10 @@ def tile_causalselfattention_pa_kernel(
                     load(16 + n)
                 if 16 <= n < 24:
                     load(n + 8)
+                if n == SINES_AT:
+                    sines()
+                if n == SINES_AT + 1:
+                    tables()
                 if n + 2 < 16:
                     widen(n + 2)
                 if n + 1 < UNITS:

@@ -41,7 +41,7 @@ X_ON_SCALAR = 2
 WV_EARLY = 3
 WV_LATE = 2
 ROTS = 8
-SINES_AT = 18
+COPY_AT = 19
 SLABS = 6
 
 
@@ -246,6 +246,8 @@ def tile_causalselfattention_pa_kernel(
         warm = const.tile([P, 1], F32, name="warm", tag="warm")
         nc.vector.memset(warm[:], 0.0)
         nc.scalar.activation(out=warm[:], in_=warm[:], func=ACT.Sin)
+        fr = const.tile([P, TB, 64], BF16, name="fr", tag="fr")
+        nc.sync.dma_start(out=fr[:], in_=freqs.rearrange("(b t) j -> t b j", t=P))
         wsc = []
         s_view = Wq_scale.rearrange("(g p j) o -> g p (j o)", p=P, j=PACK)
         for u in range(4):
@@ -259,8 +261,6 @@ def tile_causalselfattention_pa_kernel(
             xr.append(xr_t)
             for b in range(2):
                 nc.sync.dma_start(out=xr_t[:, b, :], in_=x_view[:, 2 * half + b, :])
-        fr = const.tile([P, TB, 64], BF16, name="fr", tag="fr")
-        nc.sync.dma_start(out=fr[:], in_=freqs.rearrange("(b t) j -> t b j", t=P))
         vb = const.tile([P, P], BF16, name="vb", tag="vb")
         nc.vector.memset(vb[:], 0.0)
         for v, vec in enumerate((bq, bk, gq, gk)):
@@ -284,7 +284,7 @@ def tile_causalselfattention_pa_kernel(
             if g % 2 == 0:
                 xg = slab.tile([P, 2, PACK * T], BF16, name="x_grouped", tag="slab", align_bytes=64)
             for pair in range(2):
-                xt = ps_ob.tile([P, 2, 2, P], F32, name="xt", tag="ob")
+                xt = ps_acc.tile([P, 2, 2, P], F32, name="xt", tag="acc")
                 for b in range(2):
                     words = xr[pair][:, b, :].bitcast(F32)
                     for uu in range(2):
@@ -304,7 +304,7 @@ def tile_causalselfattention_pa_kernel(
 
         vf = const.tile([P, P], F32, name="vf", tag="vf")
         nc.vector.tensor_copy(out=vf[:], in_=vb[:])
-        vp = ps_ob.tile([P, CW], F32, name="vp", tag="ob")
+        vp = ps_acc.tile([P, CW], F32, name="vp", tag="acc")
         nc.tensor.transpose(vp[:, 0:P], vf[:], ident[:])
         cols = const.tile([P, 4 * H], F32, name="cols", tag="cols")
         nc.vector.tensor_copy(out=cols[:], in_=vp[:, 0 : 4 * H])
@@ -328,6 +328,8 @@ def tile_causalselfattention_pa_kernel(
                     out=sa[:, :, :, e], in_=fr[:], func=ACT.Sin, scale=(1.0 if e == 0 else -1.0)
                 )
 
+        tps = []
+
         def tables():
             for s, src_t in enumerate((ca, sa)):
                 tp = ps_ob.tile([P, T], F32, name="tp", tag="ob")
@@ -337,7 +339,14 @@ def tile_causalselfattention_pa_kernel(
                         src_t[:, tb, :, :].rearrange("p j e -> p (j e)"),
                         ident[:],
                     )
-                nc.scalar.copy(out=tab[:, s, :], in_=tp[:])
+                tps.append(tp)
+
+        def copy_tables():
+            for s in range(2):
+                nc.scalar.copy(out=tab[:, s, :], in_=tps[s][:])
+
+        sines()
+        tables()
 
         rstd = const.tile([P, 2 * TB], F32, name="rstd", tag="rstd")
         ssr = const.tile([P, 2 * TB], F32, name="ssr", tag="ssr")
@@ -373,10 +382,8 @@ def tile_causalselfattention_pa_kernel(
                     load(16 + n)
                 if 16 <= n < 24:
                     load(n + 8)
-                if n == SINES_AT:
-                    sines()
-                if n == SINES_AT + 1:
-                    tables()
+                if n == COPY_AT:
+                    copy_tables()
                 if n + 2 < 16:
                     widen(n + 2)
                 if n + 1 < UNITS:

@@ -284,7 +284,9 @@ def tile_causalselfattention_pa_kernel(
             if g % 2 == 0:
                 xg = slab.tile([P, 2, PACK * T], BF16, name="x_grouped", tag="slab", align_bytes=64)
             for pair in range(2):
-                xt = ps_acc.tile([P, 2, 2, P], F32, name="xt", tag="acc")
+                spare = {4: (ps_ob, "ob"), 5: (ps_ss, "ss")}
+                pool_x, tag_x = spare.get(2 * g + pair, (ps_acc, "acc"))
+                xt = pool_x.tile([P, 2, 2, P], F32, name="xt", tag=tag_x)
                 for b in range(2):
                     words = xr[pair][:, b, :].bitcast(F32)
                     for uu in range(2):

@@ -384,17 +384,17 @@ def tile_causalselfattention_pa_kernel(
                     load(16 + n)
                 if 16 <= n < 24:
                     load(n + 8)
+                for w in range(2):
+                    if n == n_norm[w]:
+                        norm(w)
+                for r in finish_at.get(n, []):
+                    finish(r)
                 if n == COPY_AT:
                     copy_tables()
                 if n + 2 < 16:
                     widen(n + 2)
                 if n + 1 < UNITS:
                     interleave(n + 1)
-                for w in range(2):
-                    if n == n_norm[w]:
-                        norm(w)
-                for r in finish_at.get(n, []):
-                    finish(r)
                 for r in turn_at.get(n, []):
                     turn(r)
                 if n % 2 == 0 and 0 <= n - LAG_SQUARES < HEADS:

@@ -59,9 +59,9 @@ def tile_causalselfattention_pa_kernel(
         cpool = ctx.enter_context(tc.tile_pool(name="cpool", bufs=3))
         spool = ctx.enter_context(tc.tile_pool(name="spool", bufs=5))
         opool = ctx.enter_context(tc.tile_pool(name="opool", bufs=8))
-        ps_acc = ctx.enter_context(tc.psum_pool(name="ps_acc", bufs=4))
+        ps_acc = ctx.enter_context(tc.psum_pool(name="ps_acc", bufs=3))
         ps_ob = ctx.enter_context(tc.psum_pool(name="ps_ob", bufs=OB_BANKS))
-        ps_ss = ctx.enter_context(tc.psum_pool(name="ps_ss", bufs=1))
+        ps_ss = ctx.enter_context(tc.psum_pool(name="ps_ss", bufs=2))
 
         q_view = Wq_bytes.rearrange("(g p j) n -> g p j n", p=P, j=PACK)
         k_view = Wk.rearrange("(g p j) n -> g p j n", p=P, j=PACK)
@@ -284,7 +284,7 @@ def tile_causalselfattention_pa_kernel(
             if g % 2 == 0:
                 xg = slab.tile([P, 2, PACK * T], BF16, name="x_grouped", tag="slab", align_bytes=64)
             for pair in range(2):
-                spare = {4: (ps_ob, "ob"), 5: (ps_ss, "ss")}
+                spare = {3: (ps_ss, "ss"), 4: (ps_ob, "ob"), 5: (ps_ss, "ss")}
                 pool_x, tag_x = spare.get(2 * g + pair, (ps_acc, "acc"))
                 xt = pool_x.tile([P, 2, 2, P], F32, name="xt", tag=tag_x)
                 for b in range(2):

@@ -36,7 +36,7 @@ LAG_READ = 5
 LAG_SQUARES = 8
 FIRST_ROTATE = 21
 OB_BANKS = 3
-K_ON_SCALAR = 4
+K_ON_SCALAR = 3
 X_ON_SCALAR = 2
 WV_EARLY = 3
 WV_LATE = 2

from contextlib import ExitStack

import concourse.mybir as mybir
from concourse.masks import make_identity

F32 = mybir.dt.float32
BF16 = mybir.dt.bfloat16
U32 = mybir.dt.uint32
U8 = mybir.dt.uint8
FP8 = mybir.dt.float8_e4m3fn
FP8X4 = mybir.dt.float8_e4m3fn_x4
ACT = mybir.ActivationFunctionType
ALU = mybir.AluOpType
AX = mybir.AxisListType

T = 512
DIM = 2048
DQ = 2048
H = 16
EPS = 1e-6
HALF_PI = 1.5707963267948966
P = 128
PACK = 4
G = DIM // (P * PACK)
TB = T // P
CW = 512
HC = CW // P
NCH = DQ // CW
UNITS = 2 * NCH * G
HEADS = 2 * H

FLOPS = 2 * T * DIM * 2 * DQ

LAG_PROJECT = 4
LAG_READ = 5
LAG_SQUARES = 8
FIRST_ROTATE = 21
OB_BANKS = 3
K_ON_SCALAR = 3
X_ON_SCALAR = 2
WV_EARLY = 3
WV_LATE = 2
ROTS = 8
COPY_AT = 19
SLABS = 6


def tile_causalselfattention_pa_kernel(
    tc, x, freqs, Wq_bytes, Wq_scale, bq, Wk, bk, gq, gk, out_0, out_1
):
    nc = tc.nc
    with ExitStack() as ctx:
        const = ctx.enter_context(tc.tile_pool(name="const", bufs=1))
        slab = ctx.enter_context(tc.tile_pool(name="slab", bufs=SLABS))
        rpool = ctx.enter_context(tc.tile_pool(name="rpool", bufs=ROTS))
        qpool = ctx.enter_context(tc.tile_pool(name="qpool", bufs=8))
        kpool = ctx.enter_context(tc.tile_pool(name="kpool", bufs=8))
        stage = ctx.enter_context(tc.tile_pool(name="stage", bufs=3))
        cpool = ctx.enter_context(tc.tile_pool(name="cpool", bufs=3))
        spool = ctx.enter_context(tc.tile_pool(name="spool", bufs=5))
        opool = ctx.enter_context(tc.tile_pool(name="opool", bufs=8))
        ps_acc = ctx.enter_context(tc.psum_pool(name="ps_acc", bufs=3))
        ps_ob = ctx.enter_context(tc.psum_pool(name="ps_ob", bufs=OB_BANKS))
        ps_ss = ctx.enter_context(tc.psum_pool(name="ps_ss", bufs=2))

        q_view = Wq_bytes.rearrange("(g p j) n -> g p j n", p=P, j=PACK)
        k_view = Wk.rearrange("(g p j) n -> g p j n", p=P, j=PACK)
        x_view = x.rearrange("o (b t) k -> t (o b) k", t=P)
        out_views = (
            out_0.rearrange("o t h d -> (o t) (h d)"),
            out_1.rearrange("o t h d -> (o t) (h d)"),
        )

        raw = {}
        wide = {}
        grouped = {}
        codes = {}
        ys = {}
        sqs = {}
        rots = {}
        sums = {}
        obs = {}
        accs = {}

        def unit_place(u):
            return u // (NCH * G), (u // G) % NCH, u % G

        def load(u):
            w, c, g = unit_place(u)
            ns = slice(c * CW, (c + 1) * CW)
            if w == 0:
                t = qpool.tile([P, PACK, CW], U8, name="wq_bytes_sb", tag="wq_bytes_sb")
                nc.sync.dma_start(out=t[:], in_=q_view[g][:, :, ns])
            else:
                t = kpool.tile([P, PACK, CW], BF16, name="wk_sb", tag="wk_sb")
                nc.sync.dma_start(out=t[:], in_=k_view[g][:, :, ns])
            raw[u] = t

        def widen_on_vector(u, j):
            if u == 0:
                return True
            share = WV_EARLY if u < FIRST_ROTATE else WV_LATE
            return j >= PACK - (share + u % 2) // 2

        def widen(u):
            w, c, g = unit_place(u)
            t = stage.tile([P, PACK, CW], BF16, name="wide", tag="wide")
            for j in range(PACK):
                src = raw[u][:, j, :].bitcast(FP8)
                sc = wsc[g][:, j : j + 1]
                if widen_on_vector(u, j):
                    nc.vector.tensor_scalar(
                        out=t[:, j, :], in0=src, scalar1=sc, scalar2=None, op0=ALU.mult
                    )
                else:
                    nc.scalar.activation(out=t[:, j, :], in_=src, func=ACT.Copy, scale=sc)
            wide[u] = t

        def interleave(u):
            w, c, g = unit_place(u)
            src = wide[u] if w == 0 else raw[u]
            t = stage.tile([P, CW, PACK], BF16, name="grouped", tag="grouped", align_bytes=64)
            dst_v = t[:].rearrange("p (c i) j -> p c j i", i=4)
            src_v = src[:].rearrange("p j (c i) -> p c j i", i=4)
            if w == 1 and ((u % 16 + 1) * K_ON_SCALAR) % 16 < K_ON_SCALAR:
                nc.scalar.copy(out=dst_v, in_=src_v)
            else:
                nc.vector.tensor_copy(out=dst_v, in_=src_v)
            grouped[u] = t

        def quantize(u):
            w, c, g = unit_place(u)
            if g == 0:
                wc = cpool.tile([P, G, CW], U32, name="w_codes", tag="w_codes", align_bytes=64)
                ws = cpool.tile([P, G, CW], U8, name="w_scales", tag="w_scales", align_bytes=64)
                codes[(w, c)] = (wc, ws)
            wc, ws = codes[(w, c)]
            nc.vector.quantize_mx(
                out=wc[:, g, :].bitcast(FP8X4),
                scales=ws[:, g, :],
                in_=grouped[u][:].rearrange("p n j -> p (n j)"),
            )

        def project(hh):
            w, h = hh // H, hh % H
            c, hl = h // HC, h % HC
            wc, ws = codes[(w, c)]
            cs = slice(hl * P, (hl + 1) * P)
            acc = ps_acc.tile([P, T], F32, name="acc", tag="acc")
            for g in range(G):
                nc.tensor.matmul_mx(
                    out=acc[:],
                    lhsT=wc[:, g, cs].bitcast(FP8X4),
                    lhsT_scale=ws[:, g, cs],
                    rhs=xc[:, g, :].bitcast(FP8X4),
                    rhs_scale=xs[:, g, :],
                    start=(g == 0),
                    stop=(g == G - 1),
                )
            accs[hh] = acc

        def read_bank(hh):
            w, h = hh // H, hh % H
            c, hl = h // HC, h % HC
            acc = accs[hh]
            sq = spool.tile([P, T], F32, name="sq", tag="sq")
            nc.scalar.activation(
                out=sq[:], in_=acc[:], func=ACT.Square, scale=1.0, bias=cols[:, hh : hh + 1]
            )
            if hl == 0:
                ys[(w, c)] = slab.tile([P, HC, T], F32, name="y", tag="slab", align_bytes=64)
            nc.scalar.activation(
                out=ys[(w, c)][:, hl, :], in_=acc[:], func=ACT.Identity,
                scale=cols[:, 2 * H + hh : 2 * H + hh + 1], bias=gb[:, hh : hh + 1],
            )
            sqs[hh] = sq

        def rotate(r):
            w, c, tb = r // (NCH * TB), (r // TB) % NCH, r % TB
            ts = slice(tb * P, (tb + 1) * P)
            rot = rpool.tile([P, HC, 2, P], F32, name="rot", tag="rot")
            nc.vector.tensor_tensor(
                out=rot[:],
                in0=ys[(w, c)][:, :, ts].unsqueeze(2).to_broadcast([P, HC, 2, P]),
                in1=tab[:, :, ts].unsqueeze(1).to_broadcast([P, HC, 2, P]),
                op=ALU.mult,
            )
            rots[r] = rot

        def add_squares(hh):
            w, h = hh // H, hh % H
            if h == 0:
                sums[w] = ps_ss.tile([P, TB, P], F32, name="ss", tag="ss")
            for tb in range(TB):
                nc.tensor.matmul(
                    out=sums[w][:, tb, :],
                    lhsT=sqs[hh][:, tb * P : (tb + 1) * P],
                    rhs=ident[:],
                    is_transpose=True,
                    start=(h == 0 and tb == 0),
                    stop=(h == H - 1 and tb == TB - 1),
                )

        def norm(w):
            for tb in range(TB):
                nc.scalar.activation(
                    out=junk[:], in_=sums[w][:, tb, :], func=ACT.Copy,
                    accum_out=ssr[:, w * TB + tb : w * TB + tb + 1],
                )
            span = slice(w * TB, (w + 1) * TB)
            nc.scalar.activation(
                out=rstd[:, span], in_=ssr[:, span], func=ACT.Abs_reciprocal_sqrt,
                scale=1.0 / DQ, bias=EPS,
            )

        def turn(r):
            w, c, tb = r // (NCH * TB), (r // TB) % NCH, r % TB
            rot = rots[r]
            ob = ps_ob.tile([P, CW], F32, name="ob", tag="ob")
            for hl in range(HC):
                dst = ob[:, hl * P : (hl + 1) * P]
                nc.tensor.matmul(
                    out=dst, lhsT=rot[:, hl, 0, :], rhs=ident[:],
                    is_transpose=True, start=True, stop=False,
                )
                nc.tensor.matmul(
                    out=dst, lhsT=rot[:, hl, 1, :], rhs=swap[:],
                    is_transpose=True, start=False, stop=True,
                )
            obs[r] = ob

        def finish(r):
            w, c, tb = r // (NCH * TB), (r // TB) % NCH, r % TB
            o = opool.tile([P, CW], F32, name="osb", tag="osb")
            rs = rstd[:, w * TB + tb : w * TB + tb + 1]
            if r >= 28 and r % 2 == 1:
                nc.vector.tensor_scalar(
                    out=o[:], in0=obs[r][:], scalar1=rs, scalar2=None, op0=ALU.mult
                )
            else:
                nc.scalar.activation(out=o[:], in_=obs[r][:], func=ACT.Copy, scale=rs)
            nc.sync.dma_start(
                out=out_views[w][tb * P : (tb + 1) * P, c * CW : (c + 1) * CW], in_=o[:]
            )

        warm = const.tile([P, 1], F32, name="warm", tag="warm")
        nc.vector.memset(warm[:], 0.0)
        nc.scalar.activation(out=warm[:], in_=warm[:], func=ACT.Sin)
        fr = const.tile([P, TB, 64], BF16, name="fr", tag="fr")
        nc.sync.dma_start(out=fr[:], in_=freqs.rearrange("(b t) j -> t b j", t=P))
        wsc = []
        s_view = Wq_scale.rearrange("(g p j) o -> g p (j o)", p=P, j=PACK)
        for u in range(4):
            wsc_g = const.tile([P, 2 * PACK], F32, name="wsc", tag="wsc%d" % u)
            nc.sync.dma_start(out=wsc_g[:, 0:PACK], in_=s_view[u])
            wsc.append(wsc_g)
            load(u)
        xr = []
        for half in range(2):
            xr_t = slab.tile([P, 2, DIM], BF16, name="x_raw", tag="slab", align_bytes=64)
            xr.append(xr_t)
            for b in range(2):
                nc.sync.dma_start(out=xr_t[:, b, :], in_=x_view[:, 2 * half + b, :])
        vb = const.tile([P, P], BF16, name="vb", tag="vb")
        nc.vector.memset(vb[:], 0.0)
        for v, vec in enumerate((bq, bk, gq, gk)):
            nc.sync.dma_start(
                out=vb[H * v : H * (v + 1), :], in_=vec.rearrange("(h c) -> h c", c=P)
            )
        for u in range(4, 8):
            load(u)

        ident = const.tile([P, P], F32, name="ident", tag="ident")
        make_identity(nc, ident[:])
        swap = const.tile([P, P], F32, name="swap", tag="swap")
        iv = ident[:].rearrange("p (j e) -> p j e", e=2)
        sv = swap[:].rearrange("p (j e) -> p j e", e=2)
        nc.vector.tensor_copy(out=sv[:, :, 0], in_=iv[:, :, 1])
        nc.vector.tensor_copy(out=sv[:, :, 1], in_=iv[:, :, 0])

        xc = const.tile([P, G, T], U32, name="x_codes", tag="x_codes", align_bytes=64)
        xs = const.tile([P, G, T], U8, name="x_scales", tag="x_scales", align_bytes=64)
        for g in range(G):
            if g % 2 == 0:
                xg = slab.tile([P, 2, PACK * T], BF16, name="x_grouped", tag="slab", align_bytes=64)
            for pair in range(2):
                spare = {3: (ps_ss, "ss"), 4: (ps_ob, "ob"), 5: (ps_ss, "ss")}
                pool_x, tag_x = spare.get(2 * g + pair, (ps_acc, "acc"))
                xt = pool_x.tile([P, 2, 2, P], F32, name="xt", tag=tag_x)
                for b in range(2):
                    words = xr[pair][:, b, :].bitcast(F32)
                    for uu in range(2):
                        nc.tensor.transpose(
                            xt[:, b, uu, :], words[:, 256 * g + uu : 256 * (g + 1) : 2], ident[:]
                        )
                dst = xg[:, g % 2, :].bitcast(F32).rearrange("p (b t u) -> p b t u", b=TB, u=2)
                dst = dst[:, 2 * pair : 2 * pair + 2, :, :]
                src = xt[:].rearrange("p b u t -> p b t u")
                if pair >= X_ON_SCALAR:
                    nc.vector.tensor_copy(out=dst, in_=src)
                else:
                    nc.scalar.copy(out=dst, in_=src)
            nc.vector.quantize_mx(
                out=xc[:, g, :].bitcast(FP8X4), scales=xs[:, g, :], in_=xg[:, g % 2, :]
            )

        vf = const.tile([P, P], F32, name="vf", tag="vf")
        nc.vector.tensor_copy(out=vf[:], in_=vb[:])
        vp = ps_acc.tile([P, CW], F32, name="vp", tag="acc")
        nc.tensor.transpose(vp[:, 0:P], vf[:], ident[:])
        cols = const.tile([P, 4 * H], F32, name="cols", tag="cols")
        nc.vector.tensor_copy(out=cols[:], in_=vp[:, 0 : 4 * H])
        gb = const.tile([P, 2 * H], F32, name="gb", tag="gb")
        nc.vector.tensor_tensor(
            out=gb[:], in0=cols[:, 2 * H : 4 * H], in1=cols[:, 0 : 2 * H], op=ALU.mult
        )

        af = const.tile([P, TB, 64], F32, name="af", tag="af")
        ca = const.tile([P, TB, 64, 2], F32, name="ca", tag="ca")
        sa = const.tile([P, TB, 64, 2], F32, name="sa", tag="sa")
        tab = const.tile([P, 2, T], F32, name="tab", tag="tab")

        def sines():
            nc.scalar.activation(out=af[:], in_=fr[:], func=ACT.Abs)
            for e in range(2):
                nc.scalar.activation(
                    out=ca[:, :, :, e], in_=af[:], func=ACT.Sin, scale=-1.0, bias=HALF_PI
                )
                nc.scalar.activation(
                    out=sa[:, :, :, e], in_=fr[:], func=ACT.Sin, scale=(1.0 if e == 0 else -1.0)
                )

        tps = []

        def tables():
            for s, src_t in enumerate((ca, sa)):
                tp = ps_ob.tile([P, T], F32, name="tp", tag="ob")
                for tb in range(TB):
                    nc.tensor.transpose(
                        tp[:, tb * P : (tb + 1) * P],
                        src_t[:, tb, :, :].rearrange("p j e -> p (j e)"),
                        ident[:],
                    )
                tps.append(tp)

        def copy_tables():
            for s in range(2):
                nc.scalar.copy(out=tab[:, s, :], in_=tps[s][:])

        sines()
        tables()

        rstd = const.tile([P, 2 * TB], F32, name="rstd", tag="rstd")
        ssr = const.tile([P, 2 * TB], F32, name="ssr", tag="ssr")
        junk = const.tile([P, P], F32, name="junk", tag="junk")

        n_norm = (H - 2 + LAG_SQUARES + 1, HEADS - 2 + LAG_SQUARES + 1)
        n_units_out = NCH * TB
        rotate_at = {}
        turn_at = {}
        finish_at = {}
        last = 0
        for r0 in range(0, 2 * n_units_out, 2):
            w = r0 // n_units_out
            for r in (r0, r0 + 1):
                n_r = max(FIRST_ROTATE + r, (r // TB) * HC + HC + LAG_READ)
                rotate_at.setdefault(n_r, []).append(r)
            n_t = max(n_r + 1, n_norm[w] - OB_BANKS + (r0 + 1) % n_units_out)
            n_t += n_t % 2
            turn_at.setdefault(n_t, []).extend((r0, r0 + 1))
            for r in (r0, r0 + 1):
                n_f = max(n_t + 1 + r - r0, n_norm[w])
                finish_at.setdefault(n_f, []).append(r)
                last = max(last, n_f)
        pinned = {mybir.EngineType.PE, mybir.EngineType.DVE, mybir.EngineType.Activation}
        with tc.manual_schedule(engines=pinned):
            widen(0)
            widen(1)
            interleave(0)
            for n in range(last + 1):
                if n + 8 < 16:
                    load(n + 8)
                if n < 8:
                    load(16 + n)
                if 16 <= n < 24:
                    load(n + 8)
                for w in range(2):
                    if n == n_norm[w]:
                        norm(w)
                for r in finish_at.get(n, []):
                    finish(r)
                if n == COPY_AT:
                    copy_tables()
                if n + 2 < 16:
                    widen(n + 2)
                if n + 1 < UNITS:
                    interleave(n + 1)
                for r in turn_at.get(n, []):
                    turn(r)
                if n % 2 == 0 and 0 <= n - LAG_SQUARES < HEADS:
                    add_squares(n - LAG_SQUARES)
                    add_squares(n - LAG_SQUARES + 1)
                if n % 2 == 0 and 0 <= n - LAG_PROJECT < HEADS:
                    project(n - LAG_PROJECT)
                    project(n - LAG_PROJECT + 1)
                if 0 <= n - LAG_READ < HEADS:
                    read_bank(n - LAG_READ)
                for r in rotate_at.get(n, []):
                    rotate(r)
                if n < UNITS:
                    quantize(n)
